import numpy as np
import ml_dtypes


def mxq(x, axis, fmt="e4m3"):
    dtype, down = {"e4m3": (ml_dtypes.float8_e4m3fn, 7), "e5m2": (ml_dtypes.float8_e5m2, 14)}[fmt]
    v = np.moveaxis(np.asarray(x, np.float32).astype(ml_dtypes.bfloat16).astype(np.float64), axis, -1)
    blocks = v.reshape(v.shape[:-1] + (-1, 32))
    amax = np.abs(blocks).max(-1, keepdims=True)
    byte = np.maximum(np.where(amax > 0, np.frexp(amax)[1] - 1 + 127, 0) - down, 1)
    scale = np.exp2(byte - 127.0)
    codes = (blocks / scale).astype(np.float32).astype(dtype).astype(np.float64)
    return np.moveaxis((codes * scale).reshape(v.shape), -1, axis)


WIDE = False


def mx_kscale(k):
    if not WIDE:
        return np.ones(k)
    levels = np.array([10, -10, 5, -5, 0])
    a = np.random.permutation(np.resize(levels, k // 512 * 4)).reshape(k // 512, 4)
    idx = np.arange(k)
    return np.exp2(a[idx // 512, idx % 128 // 32])


BF16 = ml_dtypes.bfloat16


def bf(x):
    return np.asarray(x, np.float32).astype(BF16)


def f64(x):
    return np.asarray(x).astype(np.float64)


E2M1 = np.array([0.0, 0.5, 1.0, 1.5, 2.0, 3.0, 4.0, 6.0, -0.0, -0.5, -1.0, -1.5, -2.0, -3.0, -4.0, -6.0])


def pack_weight(w, fmt):
    k, n = w.shape
    w = f64(bf(w)).reshape(k // 32, 32, n)
    amax = np.abs(w).max(1)
    if fmt == "e4m3":
        byte = np.frexp(amax)[1] - 1 + 127 - 7
    else:
        mant, ex = np.frexp(amax / 6.0)
        byte = np.where(mant > 0.5, ex, ex - 1) + 127
    byte = np.clip(np.where(amax > 0, byte, 1), 1, 254)
    scaled = (w * np.exp2(127.0 - byte)[:, None, :]).reshape(k, n).astype(np.float32)
    by_word = np.ascontiguousarray(scaled.reshape(k // 512, 128, 4, n).transpose(0, 1, 3, 2))
    if fmt == "e4m3":
        words = by_word.astype(ml_dtypes.float8_e4m3fn).view(np.uint8)
    else:
        c = by_word.astype(ml_dtypes.float4_e2m1fn).view(np.uint8) & 0xF
        words = c[..., 0::2] | (c[..., 1::2] << 4)
    return np.ascontiguousarray(words), np.ascontiguousarray(byte.astype(np.uint8).reshape(k // 512, 16, n))


def unpack_weight(words, scales, fmt):
    g, p, n, _ = words.shape
    if fmt == "e4m3":
        vals = np.ascontiguousarray(words).view(ml_dtypes.float8_e4m3fn).astype(np.float64)
    else:
        nib = np.empty((g, p, n, 4), np.uint8)
        nib[..., 0::2] = words & 0xF
        nib[..., 1::2] = words >> 4
        vals = E2M1[nib]
    vals = vals * np.repeat(np.exp2(scales.astype(np.float64) - 127.0), 8, axis=1)[..., None]
    return vals.transpose(0, 1, 3, 2).reshape(g * 512, n)


B, IN, OUT = 4096, 512, 512
FMT = "e4m3"


def sigmoid(v):
    return 1.0 / (1.0 + np.exp(-v))


def setup_inputs():
    s, t = mx_kscale(IN), mx_kscale(OUT)
    x = bf(np.random.standard_normal((B, IN)) * s)
    hx = bf(np.random.standard_normal((B, OUT)) * t)
    cy = bf(np.random.standard_normal((B, OUT)) * 0.5)
    w_ih_o_words, w_ih_o_scales = pack_weight((np.random.standard_normal((OUT, IN)) * 0.7 / np.sqrt(IN) / s).T, FMT)
    w_hh_o_words, w_hh_o_scales = pack_weight((np.random.standard_normal((OUT, OUT)) * 0.7 / np.sqrt(OUT) / t).T, FMT)
    w_po_words, w_po_scales = pack_weight((np.random.standard_normal((OUT, OUT)) * 1.5 / np.sqrt(OUT)).T, FMT)
    b_ih_o = bf(np.random.standard_normal(OUT) * 0.3)
    b_hh_o = bf(np.random.standard_normal(OUT) * 0.3)
    return {
        "x": x,
        "hx": hx,
        "cy": cy,
        "w_ih_o_words": w_ih_o_words,
        "w_ih_o_scales": w_ih_o_scales,
        "w_hh_o_words": w_hh_o_words,
        "w_hh_o_scales": w_hh_o_scales,
        "w_po_words": w_po_words,
        "w_po_scales": w_po_scales,
        "b_ih_o": b_ih_o,
        "b_hh_o": b_hh_o,
    }


def reference(x, hx, cy, w_ih_o_words, w_ih_o_scales, w_hh_o_words, w_hh_o_scales, w_po_words, w_po_scales, b_ih_o, b_hh_o):
    c = f64(cy)
    o_g = (mxq(f64(x), 1, "e4m3") @ unpack_weight(w_ih_o_words, w_ih_o_scales, FMT)) + f64(b_ih_o) + (mxq(f64(hx), 1, "e4m3") @ unpack_weight(w_hh_o_words, w_hh_o_scales, FMT)) + f64(b_hh_o)
    o_g = sigmoid(o_g + (mxq(c, 1, "e4m3") @ unpack_weight(w_po_words, w_po_scales, FMT)))
    return o_g * np.tanh(c)

@@ -1,0 +1,182 @@
+from contextlib import ExitStack
+
+import concourse.mybir as mybir
+from concourse.masks import make_identity
+
+F32 = mybir.dt.float32
+BF16 = mybir.dt.bfloat16
+I32 = mybir.dt.int32
+U32 = mybir.dt.uint32
+U8 = mybir.dt.uint8
+FP8X4 = mybir.dt.float8_e4m3fn_x4
+ADD = mybir.AluOpType.add
+MULT = mybir.AluOpType.mult
+SIGMOID = mybir.ActivationFunctionType.Sigmoid
+TANH = mybir.ActivationFunctionType.Tanh
+
+P = 128
+BATCH = 4096
+K = 512
+N = 512
+OPERANDS = 3
+PAIRS = K // 2
+ROW_TILES = 2
+ROUND_ROWS = ROW_TILES * P
+ROUNDS = BATCH // ROUND_ROWS
+
+FLOPS = 2 * BATCH * K * N * OPERANDS
+
+
+def tile_ircnn_lstmcell_pb_t_kernel(
+    tc,
+    x,
+    hx,
+    cy,
+    w_ih_o_words,
+    w_ih_o_scales,
+    w_hh_o_words,
+    w_hh_o_scales,
+    w_po_words,
+    w_po_scales,
+    b_ih_o,
+    b_hh_o,
+    out,
+):
+    nc = tc.nc
+    weight_words = (w_ih_o_words, w_hh_o_words, w_po_words)
+    weight_scales = (w_ih_o_scales, w_hh_o_scales, w_po_scales)
+
+    rows_in = [a.rearrange("(r p j) k -> r p (j k)", p=P, j=ROW_TILES) for a in (x, hx, cy)]
+    rows_out = out.rearrange("(r p j) n -> r p (j n)", p=P, j=ROW_TILES)
+
+    with ExitStack() as stack:
+        consts = stack.enter_context(tc.tile_pool(name="consts", bufs=1))
+        resident = stack.enter_context(tc.tile_pool(name="resident", bufs=ROUNDS))
+        regroup = stack.enter_context(tc.tile_pool(name="regroup", bufs=2 * OPERANDS))
+        gates = stack.enter_context(tc.tile_pool(name="gates", bufs=3))
+        results = stack.enter_context(tc.tile_pool(name="results", bufs=8))
+        psum = stack.enter_context(tc.psum_pool(name="psum", bufs=4))
+        stack.enter_context(tc.manual_schedule())
+
+        w_scales = consts.tile([P, OPERANDS, N], U8, align_bytes=64)
+        nc.vector.memset(w_scales[:].rearrange("p i n -> p (i n)").bitcast(I32), 0)
+        w_codes = consts.tile([P, OPERANDS, N], U32, align_bytes=64)
+
+        bias_rows = consts.tile([P, N], BF16)
+        nc.vector.memset(bias_rows[:], 0.0)
+        ones = consts.tile([P, P], BF16)
+        nc.vector.memset(ones[:], 1.0)
+        nc.scalar.dma_start(out=bias_rows[0:1, :], in_=b_ih_o.rearrange("(o n) -> o n", o=1))
+        nc.scalar.dma_start(out=bias_rows[1:2, :], in_=b_hh_o.rearrange("(o n) -> o n", o=1))
+
+        warm = consts.tile([P, 1], F32)
+        nc.vector.memset(warm[:], 0.0)
+        nc.scalar.activation(out=warm[:], in_=warm[:], func=SIGMOID)
+
+        ident = consts.tile([P, P], F32)
+        make_identity(nc, ident[:])
+
+        loaded = [[], [], []]
+
+        def load(r):
+            for i in range(OPERANDS):
+                rows = resident.tile([P, ROW_TILES * K], BF16, name="rows%d" % i, tag="rows%d" % i)
+                nc.sync.dma_start(out=rows[:], in_=rows_in[i][r])
+                loaded[i].append(rows)
+
+        load(0)
+        for i in range(OPERANDS):
+            scale_rows = weight_scales[i].rearrange("g q n -> (g q) n")
+            for quadrant in range(4):
+                nc.sync.dma_start(
+                    out=w_scales[32 * quadrant : 32 * quadrant + 4, i, :].bitcast(I32),
+                    in_=scale_rows[4 * quadrant : 4 * quadrant + 4, :].bitcast(I32),
+                )
+        for i in range(OPERANDS):
+            nc.sync.dma_start(
+                out=w_codes[:, i, :].bitcast(I32),
+                in_=weight_words[i].rearrange("g p n t -> (g p) (n t)").bitcast(I32),
+            )
+        for r in range(1, ROUNDS):
+            load(r)
+
+        def transpose(r):
+            banks = []
+            for i in range(OPERANDS):
+                pairs = loaded[i][r][:].bitcast(F32)
+                bank = psum.tile([P, ROW_TILES, 2, P], F32, name="bank", tag="bank")
+                for j in range(ROW_TILES):
+                    for u in range(2):
+                        nc.tensor.transpose(
+                            out=bank[:, j, u, :],
+                            in_=pairs[:, j * PAIRS + u : (j + 1) * PAIRS : 2],
+                            identity=ident[:],
+                        )
+                banks.append(bank)
+            return banks
+
+        def evacuate(banks):
+            tiles = []
+            for i in range(OPERANDS):
+                grouped = regroup.tile([P, ROW_TILES * K], BF16, name="grouped", tag="grouped", align_bytes=64)
+                dst = grouped[:].bitcast(F32).rearrange("p (j m u) -> p j m u", j=ROW_TILES, u=2)
+                src = banks[i][:].rearrange("p j u m -> p j m u")
+                if i == 0:
+                    nc.vector.tensor_copy(out=dst, in_=src)
+                else:
+                    nc.scalar.copy(out=dst, in_=src)
+                tiles.append(grouped)
+            return tiles
+
+        def quantise(tiles):
+            quantised = []
+            for i in range(OPERANDS):
+                codes = regroup.tile([P, ROUND_ROWS], U32, name="codes", tag="codes", align_bytes=64)
+                scales = regroup.tile([P, ROUND_ROWS], U8, name="scales", tag="scales", align_bytes=64)
+                nc.vector.quantize_mx(out=codes[:].bitcast(FP8X4), scales=scales[:], in_=tiles[i][:])
+                quantised.append((codes, scales))
+            return quantised
+
+        def multiply(quantised):
+            sums = []
+            for j in range(ROW_TILES):
+                acc = psum.tile([P, N], F32, name="acc", tag="acc")
+                for i in range(OPERANDS):
+                    codes, scales = quantised[i]
+                    nc.tensor.matmul_mx(
+                        out=acc[:],
+                        lhsT=codes[:, j * P : (j + 1) * P].bitcast(FP8X4),
+                        lhsT_scale=scales[:, j * P : (j + 1) * P],
+                        rhs=w_codes[:, i, :].bitcast(FP8X4),
+                        rhs_scale=w_scales[:, i, :],
+                        start=(i == 0),
+                        stop=(i == OPERANDS - 1),
+                    )
+                sums.append(acc)
+            return sums
+
+        def finish(r, sums):
+            cell = results.tile([P, ROW_TILES * N], F32, name="cell", tag="cell")
+            nc.scalar.activation(out=cell[:], in_=loaded[2][r][:], func=TANH)
+            gate = gates.tile([P, ROW_TILES * N], F32, name="gate", tag="gate")
+            for j in range(ROW_TILES):
+                cols = slice(j * N, (j + 1) * N)
+                nc.vector.tensor_tensor(out=gate[:, cols], in0=sums[j][:], in1=bias[:], op=ADD)
+                nc.scalar.activation(out=gate[:, cols], in_=gate[:, cols], func=SIGMOID)
+                nc.gpsimd.tensor_tensor(out=cell[:, cols], in0=gate[:, cols], in1=cell[:, cols], op=MULT)
+            nc.sync.dma_start(out=rows_out[r], in_=cell[:])
+
+        quantised = quantise(evacuate(transpose(0)))
+
+        bias_sum = psum.tile([P, N], F32, name="acc", tag="acc")
+        nc.tensor.matmul(out=bias_sum[:], lhsT=ones[:], rhs=bias_rows[:], start=True, stop=True)
+        bias = consts.tile([P, N], F32)
+        nc.vector.tensor_copy(out=bias[:], in_=bias_sum[:])
+
+        for r in range(ROUNDS):
+            if r + 1 < ROUNDS:
+                tiles = evacuate(transpose(r + 1))
+            sums = multiply(quantised)
+            if r + 1 < ROUNDS:
+                quantised = quantise(tiles)
+            finish(r, sums)

@@ -54,7 +54,7 @@ def tile_ircnn_lstmcell_pb_t_kernel(
         resident = stack.enter_context(tc.tile_pool(name="resident", bufs=ROUNDS))
         regroup = stack.enter_context(tc.tile_pool(name="regroup", bufs=2 * OPERANDS))
         gates = stack.enter_context(tc.tile_pool(name="gates", bufs=3))
-        results = stack.enter_context(tc.tile_pool(name="results", bufs=8))
+        results = stack.enter_context(tc.tile_pool(name="results", bufs=10))
         psum = stack.enter_context(tc.psum_pool(name="psum", bufs=4))
         stack.enter_context(tc.manual_schedule())
 
@@ -115,13 +115,13 @@ def tile_ircnn_lstmcell_pb_t_kernel(
                 banks.append(bank)
             return banks
 
-        def evacuate(banks):
+        def evacuate(r, banks):
             tiles = []
             for i in range(OPERANDS):
                 grouped = regroup.tile([P, ROW_TILES * K], BF16, name="grouped", tag="grouped", align_bytes=64)
                 dst = grouped[:].bitcast(F32).rearrange("p (j m u) -> p j m u", j=ROW_TILES, u=2)
                 src = banks[i][:].rearrange("p j u m -> p j m u")
-                if i == 0:
+                if i == 0 or (i == 1 and r % 2 == 0):
                     nc.vector.tensor_copy(out=dst, in_=src)
                 else:
                     nc.scalar.copy(out=dst, in_=src)
@@ -155,18 +155,25 @@ def tile_ircnn_lstmcell_pb_t_kernel(
                 sums.append(acc)
             return sums
 
-        def finish(r, sums):
-            cell = results.tile([P, ROW_TILES * N], F32, name="cell", tag="cell")
-            nc.scalar.activation(out=cell[:], in_=loaded[2][r][:], func=TANH)
+        def add_bias(sums):
             gate = gates.tile([P, ROW_TILES * N], F32, name="gate", tag="gate")
             for j in range(ROW_TILES):
-                cols = slice(j * N, (j + 1) * N)
-                nc.vector.tensor_tensor(out=gate[:, cols], in0=sums[j][:], in1=bias[:], op=ADD)
-                nc.scalar.activation(out=gate[:, cols], in_=gate[:, cols], func=SIGMOID)
-                nc.gpsimd.tensor_tensor(out=cell[:, cols], in0=gate[:, cols], in1=cell[:, cols], op=MULT)
-            nc.sync.dma_start(out=rows_out[r], in_=cell[:])
+                nc.vector.tensor_tensor(out=gate[:, j * N : (j + 1) * N], in0=sums[j][:], in1=bias[:], op=ADD)
+            return gate
 
-        quantised = quantise(evacuate(transpose(0)))
+        def tanh_of_cell(r):
+            cell = results.tile([P, ROW_TILES * N], F32, name="cell", tag="cell")
+            nc.scalar.activation(out=cell[:], in_=loaded[2][r][:], func=TANH)
+            return cell
+
+        def finish(r, gate, cell, multiplier):
+            for j in range(ROW_TILES):
+                cols = slice(j * N, (j + 1) * N)
+                nc.scalar.activation(out=gate[:, cols], in_=gate[:, cols], func=SIGMOID)
+                multiplier.tensor_tensor(out=cell[:, cols], in0=gate[:, cols], in1=cell[:, cols], op=MULT)
+                nc.sync.dma_start(out=rows_out[r][:, cols], in_=cell[:, cols])
+
+        quantised = quantise(evacuate(0, transpose(0)))
 
         bias_sum = psum.tile([P, N], F32, name="acc", tag="acc")
         nc.tensor.matmul(out=bias_sum[:], lhsT=ones[:], rhs=bias_rows[:], start=True, stop=True)
@@ -175,8 +182,15 @@ def tile_ircnn_lstmcell_pb_t_kernel(
 
         for r in range(ROUNDS):
             if r + 1 < ROUNDS:
-                tiles = evacuate(transpose(r + 1))
+                banks = transpose(r + 1)
+            if r > 0:
+                gate = add_bias(sums)
+            if r + 1 < ROUNDS:
+                tiles = evacuate(r + 1, banks)
             sums = multiply(quantised)
             if r + 1 < ROUNDS:
                 quantised = quantise(tiles)
-            finish(r, sums)
+            if r > 0:
+                finish(r - 1, gate, cell, nc.gpsimd)
+            cell = tanh_of_cell(r)
+        finish(ROUNDS - 1, add_bias(sums), cell, nc.vector)

@@ -66,8 +66,6 @@ def tile_ircnn_lstmcell_pb_t_kernel(
         nc.vector.memset(bias_rows[:], 0.0)
         ones = consts.tile([P, P], BF16)
         nc.vector.memset(ones[:], 1.0)
-        nc.scalar.dma_start(out=bias_rows[0:1, :], in_=b_ih_o.rearrange("(o n) -> o n", o=1))
-        nc.scalar.dma_start(out=bias_rows[1:2, :], in_=b_hh_o.rearrange("(o n) -> o n", o=1))
 
         warm = consts.tile([P, 1], F32)
         nc.vector.memset(warm[:], 0.0)
@@ -75,6 +73,14 @@ def tile_ircnn_lstmcell_pb_t_kernel(
 
         ident = consts.tile([P, P], F32)
         make_identity(nc, ident[:])
+
+        for i in range(OPERANDS):
+            nc.gpsimd.dma_start(
+                out=w_codes[:, i, :].bitcast(F32),
+                in_=weight_words[i].rearrange("g p n t -> (g p) (n t)").bitcast(F32),
+            )
+        nc.gpsimd.dma_start(out=bias_rows[0:1, :].bitcast(F32), in_=b_ih_o.rearrange("(o n) -> o n", o=1).bitcast(F32))
+        nc.gpsimd.dma_start(out=bias_rows[1:2, :].bitcast(F32), in_=b_hh_o.rearrange("(o n) -> o n", o=1).bitcast(F32))
 
         loaded = [[], [], []]
 
@@ -85,6 +91,7 @@ def tile_ircnn_lstmcell_pb_t_kernel(
                 loaded[i].append(rows)
 
         load(0)
+        load(1)
         for i in range(OPERANDS):
             scale_rows = weight_scales[i].rearrange("g q n -> (g q) n")
             for quadrant in range(4):
@@ -92,12 +99,7 @@ def tile_ircnn_lstmcell_pb_t_kernel(
                     out=w_scales[32 * quadrant : 32 * quadrant + 4, i, :].bitcast(I32),
                     in_=scale_rows[4 * quadrant : 4 * quadrant + 4, :].bitcast(I32),
                 )
-        for i in range(OPERANDS):
-            nc.sync.dma_start(
-                out=w_codes[:, i, :].bitcast(I32),
-                in_=weight_words[i].rearrange("g p n t -> (g p) (n t)").bitcast(I32),
-            )
-        for r in range(1, ROUNDS):
+        for r in range(2, ROUNDS):
             load(r)
 
         def transpose(r):
@@ -174,11 +176,7 @@ def tile_ircnn_lstmcell_pb_t_kernel(
                 nc.sync.dma_start(out=rows_out[r][:, cols], in_=cell[:, cols])
 
         quantised = quantise(evacuate(0, transpose(0)))
-
-        bias_sum = psum.tile([P, N], F32, name="acc", tag="acc")
-        nc.tensor.matmul(out=bias_sum[:], lhsT=ones[:], rhs=bias_rows[:], start=True, stop=True)
         bias = consts.tile([P, N], F32)
-        nc.vector.tensor_copy(out=bias[:], in_=bias_sum[:])
 
         for r in range(ROUNDS):
             if r + 1 < ROUNDS:
@@ -190,6 +188,10 @@ def tile_ircnn_lstmcell_pb_t_kernel(
             sums = multiply(quantised)
             if r + 1 < ROUNDS:
                 quantised = quantise(tiles)
+            if r == 0:
+                bias_sum = psum.tile([P, N], F32, name="acc", tag="acc")
+                nc.tensor.matmul(out=bias_sum[:], lhsT=ones[:], rhs=bias_rows[:], start=True, stop=True)
+                nc.vector.tensor_copy(out=bias[:], in_=bias_sum[:])
             if r > 0:
                 finish(r - 1, gate, cell, nc.gpsimd)
             cell = tanh_of_cell(r)

@@ -66,6 +66,8 @@ def tile_ircnn_lstmcell_pb_t_kernel(
         nc.vector.memset(bias_rows[:], 0.0)
         ones = consts.tile([P, P], BF16)
         nc.vector.memset(ones[:], 1.0)
+        nc.scalar.dma_start(out=bias_rows[0:1, :], in_=b_ih_o.rearrange("(o n) -> o n", o=1))
+        nc.scalar.dma_start(out=bias_rows[1:2, :], in_=b_hh_o.rearrange("(o n) -> o n", o=1))
 
         warm = consts.tile([P, 1], F32)
         nc.vector.memset(warm[:], 0.0)
@@ -79,8 +81,6 @@ def tile_ircnn_lstmcell_pb_t_kernel(
                 out=w_codes[:, i, :].bitcast(F32),
                 in_=weight_words[i].rearrange("g p n t -> (g p) (n t)").bitcast(F32),
             )
-        nc.gpsimd.dma_start(out=bias_rows[0:1, :].bitcast(F32), in_=b_ih_o.rearrange("(o n) -> o n", o=1).bitcast(F32))
-        nc.gpsimd.dma_start(out=bias_rows[1:2, :].bitcast(F32), in_=b_hh_o.rearrange("(o n) -> o n", o=1).bitcast(F32))
 
         loaded = [[], [], []]
 
@@ -177,6 +177,7 @@ def tile_ircnn_lstmcell_pb_t_kernel(
 
         quantised = quantise(evacuate(0, transpose(0)))
         bias = consts.tile([P, N], F32)
+        next_cell = tanh_of_cell(0)
 
         for r in range(ROUNDS):
             if r + 1 < ROUNDS:
@@ -194,5 +195,7 @@ def tile_ircnn_lstmcell_pb_t_kernel(
                 nc.vector.tensor_copy(out=bias[:], in_=bias_sum[:])
             if r > 0:
                 finish(r - 1, gate, cell, nc.gpsimd)
-            cell = tanh_of_cell(r)
+            cell = next_cell
+            if r + 1 < ROUNDS:
+                next_cell = tanh_of_cell(r + 1)
         finish(ROUNDS - 1, add_bias(sums), cell, nc.vector)

@@ -123,7 +123,7 @@ def tile_ircnn_lstmcell_pb_t_kernel(
                 grouped = regroup.tile([P, ROW_TILES * K], BF16, name="grouped", tag="grouped", align_bytes=64)
                 dst = grouped[:].bitcast(F32).rearrange("p (j m u) -> p j m u", j=ROW_TILES, u=2)
                 src = banks[i][:].rearrange("p j u m -> p j m u")
-                if i == 0 or (i == 1 and r % 2 == 0):
+                if i == 0:
                     nc.vector.tensor_copy(out=dst, in_=src)
                 else:
                     nc.scalar.copy(out=dst, in_=src)
@@ -168,12 +168,15 @@ def tile_ircnn_lstmcell_pb_t_kernel(
             nc.scalar.activation(out=cell[:], in_=loaded[2][r][:], func=TANH)
             return cell
 
-        def finish(r, gate, cell, multiplier):
+        def sigmoid(gate):
             for j in range(ROW_TILES):
                 cols = slice(j * N, (j + 1) * N)
                 nc.scalar.activation(out=gate[:, cols], in_=gate[:, cols], func=SIGMOID)
-                multiplier.tensor_tensor(out=cell[:, cols], in0=gate[:, cols], in1=cell[:, cols], op=MULT)
-                nc.sync.dma_start(out=rows_out[r][:, cols], in_=cell[:, cols])
+
+        def product(r, j, gate, cell, multiplier):
+            cols = slice(j * N, (j + 1) * N)
+            multiplier.tensor_tensor(out=cell[:, cols], in0=gate[:, cols], in1=cell[:, cols], op=MULT)
+            nc.sync.dma_start(out=rows_out[r][:, cols], in_=cell[:, cols])
 
         quantised = quantise(evacuate(0, transpose(0)))
         bias = consts.tile([P, N], F32)
@@ -186,6 +189,8 @@ def tile_ircnn_lstmcell_pb_t_kernel(
                 gate = add_bias(sums)
             if r + 1 < ROUNDS:
                 tiles = evacuate(r + 1, banks)
+            if r > 1:
+                product(r - 2, 1, *finishing, nc.vector)
             sums = multiply(quantised)
             if r + 1 < ROUNDS:
                 quantised = quantise(tiles)
@@ -194,8 +199,14 @@ def tile_ircnn_lstmcell_pb_t_kernel(
                 nc.tensor.matmul(out=bias_sum[:], lhsT=ones[:], rhs=bias_rows[:], start=True, stop=True)
                 nc.vector.tensor_copy(out=bias[:], in_=bias_sum[:])
             if r > 0:
-                finish(r - 1, gate, cell, nc.gpsimd)
+                sigmoid(gate)
+                product(r - 1, 0, gate, cell, nc.gpsimd)
+                finishing = (gate, cell)
             cell = next_cell
             if r + 1 < ROUNDS:
                 next_cell = tanh_of_cell(r + 1)
-        finish(ROUNDS - 1, add_bias(sums), cell, nc.vector)
+        gate = add_bias(sums)
+        product(ROUNDS - 2, 1, *finishing, nc.vector)
+        sigmoid(gate)
+        for j in range(ROW_TILES):
+            product(ROUNDS - 1, j, gate, cell, nc.vector)

@@ -23,6 +23,7 @@ PAIRS = K // 2
 ROW_TILES = 2
 ROUND_ROWS = ROW_TILES * P
 ROUNDS = BATCH // ROUND_ROWS
+SCALES_PER_LOAD = 3
 
 FLOPS = 2 * BATCH * K * N * OPERANDS
 
@@ -84,23 +85,22 @@ def tile_ircnn_lstmcell_pb_t_kernel(
 
         loaded = [[], [], []]
 
-        def load(r):
-            for i in range(OPERANDS):
-                rows = resident.tile([P, ROW_TILES * K], BF16, name="rows%d" % i, tag="rows%d" % i)
-                nc.sync.dma_start(out=rows[:], in_=rows_in[i][r])
-                loaded[i].append(rows)
+        def load(r, i):
+            rows = resident.tile([P, ROW_TILES * K], BF16, name="rows%d" % i, tag="rows%d" % i)
+            nc.sync.dma_start(out=rows[:], in_=rows_in[i][r])
+            loaded[i].append(rows)
 
-        load(0)
-        load(1)
-        for i in range(OPERANDS):
-            scale_rows = weight_scales[i].rearrange("g q n -> (g q) n")
-            for quadrant in range(4):
-                nc.sync.dma_start(
-                    out=w_scales[32 * quadrant : 32 * quadrant + 4, i, :].bitcast(I32),
-                    in_=scale_rows[4 * quadrant : 4 * quadrant + 4, :].bitcast(I32),
-                )
-        for r in range(2, ROUNDS):
-            load(r)
+        scale_parts = [(i, quadrant) for i in range(OPERANDS) for quadrant in range(4)]
+        for r in range(ROUNDS):
+            for i in range(OPERANDS):
+                load(r, i)
+                woven = scale_parts[:SCALES_PER_LOAD] if r > 0 else []
+                for w, quadrant in woven:
+                    nc.sync.dma_start(
+                        out=w_scales[32 * quadrant : 32 * quadrant + 4, w, :].bitcast(I32),
+                        in_=weight_scales[w].rearrange("g q n -> (g q) n")[4 * quadrant : 4 * quadrant + 4, :].bitcast(I32),
+                    )
+                    scale_parts.remove((w, quadrant))
 
         def transpose(r):
             banks = []
@@ -139,22 +139,22 @@ def tile_ircnn_lstmcell_pb_t_kernel(
                 quantised.append((codes, scales))
             return quantised
 
-        def multiply(quantised):
-            sums = []
-            for j in range(ROW_TILES):
-                acc = psum.tile([P, N], F32, name="acc", tag="acc")
-                for i in range(OPERANDS):
-                    codes, scales = quantised[i]
-                    nc.tensor.matmul_mx(
-                        out=acc[:],
-                        lhsT=codes[:, j * P : (j + 1) * P].bitcast(FP8X4),
-                        lhsT_scale=scales[:, j * P : (j + 1) * P],
-                        rhs=w_codes[:, i, :].bitcast(FP8X4),
-                        rhs_scale=w_scales[:, i, :],
-                        start=(i == 0),
-                        stop=(i == OPERANDS - 1),
-                    )
-                sums.append(acc)
+        def multiply(r, quantised):
+            sums = [psum.tile([P, N], F32, name="acc", tag="acc") for j in range(ROW_TILES)]
+            order = [(j, i) for j in range(ROW_TILES) for i in range(OPERANDS)]
+            if r == 0:
+                order = [(j, i) for i in range(OPERANDS) for j in range(ROW_TILES)]
+            for j, i in order:
+                codes, scales = quantised[i]
+                nc.tensor.matmul_mx(
+                    out=sums[j][:],
+                    lhsT=codes[:, j * P : (j + 1) * P].bitcast(FP8X4),
+                    lhsT_scale=scales[:, j * P : (j + 1) * P],
+                    rhs=w_codes[:, i, :].bitcast(FP8X4),
+                    rhs_scale=w_scales[:, i, :],
+                    start=(i == 0),
+                    stop=(i == OPERANDS - 1),
+                )
             return sums
 
         def add_bias(sums):
@@ -191,7 +191,7 @@ def tile_ircnn_lstmcell_pb_t_kernel(
                 tiles = evacuate(r + 1, banks)
             if r > 1:
                 product(r - 2, 1, *finishing, nc.vector)
-            sums = multiply(quantised)
+            sums = multiply(r, quantised)
             if r + 1 < ROUNDS:
                 quantised = quantise(tiles)
             if r == 0:

@@ -23,7 +23,6 @@ PAIRS = K // 2
 ROW_TILES = 2
 ROUND_ROWS = ROW_TILES * P
 ROUNDS = BATCH // ROUND_ROWS
-SCALES_PER_LOAD = 3
 
 FLOPS = 2 * BATCH * K * N * OPERANDS
 
@@ -44,10 +43,10 @@ def tile_ircnn_lstmcell_pb_t_kernel(
     out,
 ):
     nc = tc.nc
-    weight_words = (w_ih_o_words, w_hh_o_words, w_po_words)
-    weight_scales = (w_ih_o_scales, w_hh_o_scales, w_po_scales)
+    weight_words = (w_po_words, w_ih_o_words, w_hh_o_words)
+    weight_scales = (w_po_scales, w_ih_o_scales, w_hh_o_scales)
 
-    rows_in = [a.rearrange("(r p j) k -> r p (j k)", p=P, j=ROW_TILES) for a in (x, hx, cy)]
+    rows_in = [a.rearrange("(r p j) k -> r p (j k)", p=P, j=ROW_TILES) for a in (cy, x, hx)]
     rows_out = out.rearrange("(r p j) n -> r p (j n)", p=P, j=ROW_TILES)
 
     with ExitStack() as stack:
@@ -59,20 +58,19 @@ def tile_ircnn_lstmcell_pb_t_kernel(
         psum = stack.enter_context(tc.psum_pool(name="psum", bufs=4))
         stack.enter_context(tc.manual_schedule())
 
-        w_scales = consts.tile([P, OPERANDS, N], U8, align_bytes=64)
-        nc.vector.memset(w_scales[:].rearrange("p i n -> p (i n)").bitcast(I32), 0)
-        w_codes = consts.tile([P, OPERANDS, N], U32, align_bytes=64)
-
         bias_rows = consts.tile([P, N], BF16)
         nc.vector.memset(bias_rows[:], 0.0)
         ones = consts.tile([P, P], BF16)
-        nc.vector.memset(ones[:], 1.0)
-        nc.scalar.dma_start(out=bias_rows[0:1, :], in_=b_ih_o.rearrange("(o n) -> o n", o=1))
-        nc.scalar.dma_start(out=bias_rows[1:2, :], in_=b_hh_o.rearrange("(o n) -> o n", o=1))
 
         warm = consts.tile([P, 1], F32)
-        nc.vector.memset(warm[:], 0.0)
+        nc.gpsimd.memset(warm[:], 0.0)
         nc.scalar.activation(out=warm[:], in_=warm[:], func=SIGMOID)
+
+        w_scales = consts.tile([P, OPERANDS, N], U8, align_bytes=64)
+        nc.gpsimd.memset(w_scales[:].rearrange("p i n -> p (i n)").bitcast(I32), 0)
+        w_codes = consts.tile([P, OPERANDS, N], U32, align_bytes=64)
+
+        nc.vector.memset(ones[:], 1.0)
 
         ident = consts.tile([P, P], F32)
         make_identity(nc, ident[:])
@@ -85,22 +83,25 @@ def tile_ircnn_lstmcell_pb_t_kernel(
 
         loaded = [[], [], []]
 
-        def load(r, i):
-            rows = resident.tile([P, ROW_TILES * K], BF16, name="rows%d" % i, tag="rows%d" % i)
-            nc.sync.dma_start(out=rows[:], in_=rows_in[i][r])
-            loaded[i].append(rows)
-
-        scale_parts = [(i, quadrant) for i in range(OPERANDS) for quadrant in range(4)]
-        for r in range(ROUNDS):
+        def load(r):
             for i in range(OPERANDS):
-                load(r, i)
-                woven = scale_parts[:SCALES_PER_LOAD] if r > 0 else []
-                for w, quadrant in woven:
-                    nc.sync.dma_start(
-                        out=w_scales[32 * quadrant : 32 * quadrant + 4, w, :].bitcast(I32),
-                        in_=weight_scales[w].rearrange("g q n -> (g q) n")[4 * quadrant : 4 * quadrant + 4, :].bitcast(I32),
-                    )
-                    scale_parts.remove((w, quadrant))
+                rows = resident.tile([P, ROW_TILES * K], BF16, name="rows%d" % i, tag="rows%d" % i)
+                nc.sync.dma_start(out=rows[:], in_=rows_in[i][r])
+                loaded[i].append(rows)
+
+        load(0)
+        load(1)
+        for i in range(OPERANDS):
+            scale_rows = weight_scales[i].rearrange("g q n -> (g q) n")
+            for quadrant in range(4):
+                nc.sync.dma_start(
+                    out=w_scales[32 * quadrant : 32 * quadrant + 4, i, :].bitcast(I32),
+                    in_=scale_rows[4 * quadrant : 4 * quadrant + 4, :].bitcast(I32),
+                )
+        for n, b in enumerate((b_ih_o, b_hh_o)):
+            nc.sync.dma_start(out=bias_rows[n : n + 1, :], in_=b.rearrange("(o n) -> o n", o=1))
+        for r in range(2, ROUNDS):
+            load(r)
 
         def transpose(r):
             banks = []
@@ -123,7 +124,7 @@ def tile_ircnn_lstmcell_pb_t_kernel(
                 grouped = regroup.tile([P, ROW_TILES * K], BF16, name="grouped", tag="grouped", align_bytes=64)
                 dst = grouped[:].bitcast(F32).rearrange("p (j m u) -> p j m u", j=ROW_TILES, u=2)
                 src = banks[i][:].rearrange("p j u m -> p j m u")
-                if i == 0:
+                if i == 1:
                     nc.vector.tensor_copy(out=dst, in_=src)
                 else:
                     nc.scalar.copy(out=dst, in_=src)
@@ -139,23 +140,20 @@ def tile_ircnn_lstmcell_pb_t_kernel(
                 quantised.append((codes, scales))
             return quantised
 
-        def multiply(r, quantised):
-            sums = [psum.tile([P, N], F32, name="acc", tag="acc") for j in range(ROW_TILES)]
-            order = [(j, i) for j in range(ROW_TILES) for i in range(OPERANDS)]
-            if r == 0:
-                order = [(j, i) for i in range(OPERANDS) for j in range(ROW_TILES)]
-            for j, i in order:
+        def multiply(quantised, j, cols):
+            acc = psum.tile([P, cols.stop - cols.start], F32, name="acc", tag="acc")
+            for i in range(OPERANDS):
                 codes, scales = quantised[i]
                 nc.tensor.matmul_mx(
-                    out=sums[j][:],
+                    out=acc[:],
                     lhsT=codes[:, j * P : (j + 1) * P].bitcast(FP8X4),
                     lhsT_scale=scales[:, j * P : (j + 1) * P],
-                    rhs=w_codes[:, i, :].bitcast(FP8X4),
-                    rhs_scale=w_scales[:, i, :],
+                    rhs=w_codes[:, i, cols].bitcast(FP8X4),
+                    rhs_scale=w_scales[:, i, cols],
                     start=(i == 0),
                     stop=(i == OPERANDS - 1),
                 )
-            return sums
+            return acc
 
         def add_bias(sums):
             gate = gates.tile([P, ROW_TILES * N], F32, name="gate", tag="gate")
@@ -165,7 +163,7 @@ def tile_ircnn_lstmcell_pb_t_kernel(
 
         def tanh_of_cell(r):
             cell = results.tile([P, ROW_TILES * N], F32, name="cell", tag="cell")
-            nc.scalar.activation(out=cell[:], in_=loaded[2][r][:], func=TANH)
+            nc.scalar.activation(out=cell[:], in_=loaded[0][r][:], func=TANH)
             return cell
 
         def sigmoid(gate):
@@ -178,20 +176,25 @@ def tile_ircnn_lstmcell_pb_t_kernel(
             multiplier.tensor_tensor(out=cell[:, cols], in0=gate[:, cols], in1=cell[:, cols], op=MULT)
             nc.sync.dma_start(out=rows_out[r][:, cols], in_=cell[:, cols])
 
+        whole_tiles = [(j, slice(0, N)) for j in range(ROW_TILES)]
+        last_pieces = whole_tiles[:-1] + [(ROW_TILES - 1, slice(h * N // 2, (h + 1) * N // 2)) for h in range(2)]
+
+        cells = [tanh_of_cell(0)]
         quantised = quantise(evacuate(0, transpose(0)))
         bias = consts.tile([P, N], F32)
-        next_cell = tanh_of_cell(0)
 
         for r in range(ROUNDS):
             if r + 1 < ROUNDS:
                 banks = transpose(r + 1)
+                cells.append(tanh_of_cell(r + 1))
             if r > 0:
                 gate = add_bias(sums)
             if r + 1 < ROUNDS:
                 tiles = evacuate(r + 1, banks)
             if r > 1:
                 product(r - 2, 1, *finishing, nc.vector)
-            sums = multiply(r, quantised)
+            pieces = whole_tiles if r + 1 < ROUNDS else last_pieces
+            sums = [multiply(quantised, j, cols) for j, cols in pieces]
             if r + 1 < ROUNDS:
                 quantised = quantise(tiles)
             if r == 0:
@@ -200,13 +203,15 @@ def tile_ircnn_lstmcell_pb_t_kernel(
                 nc.vector.tensor_copy(out=bias[:], in_=bias_sum[:])
             if r > 0:
                 sigmoid(gate)
-                product(r - 1, 0, gate, cell, nc.gpsimd)
-                finishing = (gate, cell)
-            cell = next_cell
-            if r + 1 < ROUNDS:
-                next_cell = tanh_of_cell(r + 1)
-        gate = add_bias(sums)
+                product(r - 1, 0, gate, cells[r - 1], nc.gpsimd)
+                finishing = (gate, cells[r - 1])
+        gate = gates.tile([P, ROW_TILES * N], F32, name="gate", tag="gate")
+        places = [slice(j * N + cols.start, j * N + cols.stop) for j, cols in last_pieces]
+        for acc, (j, cols), there in zip(sums, last_pieces, places):
+            nc.vector.tensor_tensor(out=gate[:, there], in0=acc[:], in1=bias[:, cols], op=ADD)
+            nc.scalar.activation(out=gate[:, there], in_=gate[:, there], func=SIGMOID)
         product(ROUNDS - 2, 1, *finishing, nc.vector)
-        sigmoid(gate)
-        for j in range(ROW_TILES):
-            product(ROUNDS - 1, j, gate, cell, nc.vector)
+        cell = cells[ROUNDS - 1]
+        for there in places:
+            nc.vector.tensor_tensor(out=cell[:, there], in0=gate[:, there], in1=cell[:, there], op=MULT)
+            nc.sync.dma_start(out=rows_out[ROUNDS - 1][:, there], in_=cell[:, there])

from contextlib import ExitStack

import concourse.mybir as mybir
from concourse.masks import make_identity

F32 = mybir.dt.float32
BF16 = mybir.dt.bfloat16
I32 = mybir.dt.int32
U32 = mybir.dt.uint32
U8 = mybir.dt.uint8
FP8X4 = mybir.dt.float8_e4m3fn_x4
ADD = mybir.AluOpType.add
MULT = mybir.AluOpType.mult
SIGMOID = mybir.ActivationFunctionType.Sigmoid
TANH = mybir.ActivationFunctionType.Tanh

P = 128
BATCH = 4096
K = 512
N = 512
OPERANDS = 3
PAIRS = K // 2
ROW_TILES = 2
ROUND_ROWS = ROW_TILES * P
ROUNDS = BATCH // ROUND_ROWS

FLOPS = 2 * BATCH * K * N * OPERANDS


def tile_ircnn_lstmcell_pb_t_kernel(
    tc,
    x,
    hx,
    cy,
    w_ih_o_words,
    w_ih_o_scales,
    w_hh_o_words,
    w_hh_o_scales,
    w_po_words,
    w_po_scales,
    b_ih_o,
    b_hh_o,
    out,
):
    nc = tc.nc
    weight_words = (w_po_words, w_ih_o_words, w_hh_o_words)
    weight_scales = (w_po_scales, w_ih_o_scales, w_hh_o_scales)

    rows_in = [a.rearrange("(r p j) k -> r p (j k)", p=P, j=ROW_TILES) for a in (cy, x, hx)]
    rows_out = out.rearrange("(r p j) n -> r p (j n)", p=P, j=ROW_TILES)

    with ExitStack() as stack:
        consts = stack.enter_context(tc.tile_pool(name="consts", bufs=1))
        resident = stack.enter_context(tc.tile_pool(name="resident", bufs=ROUNDS))
        regroup = stack.enter_context(tc.tile_pool(name="regroup", bufs=2 * OPERANDS))
        gates = stack.enter_context(tc.tile_pool(name="gates", bufs=3))
        results = stack.enter_context(tc.tile_pool(name="results", bufs=10))
        psum = stack.enter_context(tc.psum_pool(name="psum", bufs=4))
        stack.enter_context(tc.manual_schedule())

        bias_rows = consts.tile([P, N], BF16)
        nc.vector.memset(bias_rows[:], 0.0)
        ones = consts.tile([P, P], BF16)

        warm = consts.tile([P, 1], F32)
        nc.gpsimd.memset(warm[:], 0.0)
        nc.scalar.activation(out=warm[:], in_=warm[:], func=SIGMOID)

        w_scales = consts.tile([P, OPERANDS, N], U8, align_bytes=64)
        nc.gpsimd.memset(w_scales[:].rearrange("p i n -> p (i n)").bitcast(I32), 0)
        w_codes = consts.tile([P, OPERANDS, N], U32, align_bytes=64)

        nc.vector.memset(ones[:], 1.0)

        ident = consts.tile([P, P], F32)
        make_identity(nc, ident[:])

        for i in range(OPERANDS):
            nc.gpsimd.dma_start(
                out=w_codes[:, i, :].bitcast(F32),
                in_=weight_words[i].rearrange("g p n t -> (g p) (n t)").bitcast(F32),
            )

        loaded = [[], [], []]

        def load(r):
            for i in range(OPERANDS):
                rows = resident.tile([P, ROW_TILES * K], BF16, name="rows%d" % i, tag="rows%d" % i)
                nc.sync.dma_start(out=rows[:], in_=rows_in[i][r])
                loaded[i].append(rows)

        load(0)
        load(1)
        for i in range(OPERANDS):
            scale_rows = weight_scales[i].rearrange("g q n -> (g q) n")
            for quadrant in range(4):
                nc.sync.dma_start(
                    out=w_scales[32 * quadrant : 32 * quadrant + 4, i, :].bitcast(I32),
                    in_=scale_rows[4 * quadrant : 4 * quadrant + 4, :].bitcast(I32),
                )
        for n, b in enumerate((b_ih_o, b_hh_o)):
            nc.sync.dma_start(out=bias_rows[n : n + 1, :], in_=b.rearrange("(o n) -> o n", o=1))
        for r in range(2, ROUNDS):
            load(r)

        def transpose(r):
            banks = []
            for i in range(OPERANDS):
                pairs = loaded[i][r][:].bitcast(F32)
                bank = psum.tile([P, ROW_TILES, 2, P], F32, name="bank", tag="bank")
                for j in range(ROW_TILES):
                    for u in range(2):
                        nc.tensor.transpose(
                            out=bank[:, j, u, :],
                            in_=pairs[:, j * PAIRS + u : (j + 1) * PAIRS : 2],
                            identity=ident[:],
                        )
                banks.append(bank)
            return banks

        def evacuate(r, banks):
            tiles = []
            for i in range(OPERANDS):
                grouped = regroup.tile([P, ROW_TILES * K], BF16, name="grouped", tag="grouped", align_bytes=64)
                dst = grouped[:].bitcast(F32).rearrange("p (j m u) -> p j m u", j=ROW_TILES, u=2)
                src = banks[i][:].rearrange("p j u m -> p j m u")
                if i == 1:
                    nc.vector.tensor_copy(out=dst, in_=src)
                else:
                    nc.scalar.copy(out=dst, in_=src)
                tiles.append(grouped)
            return tiles

        def quantise(tiles):
            quantised = []
            for i in range(OPERANDS):
                codes = regroup.tile([P, ROUND_ROWS], U32, name="codes", tag="codes", align_bytes=64)
                scales = regroup.tile([P, ROUND_ROWS], U8, name="scales", tag="scales", align_bytes=64)
                nc.vector.quantize_mx(out=codes[:].bitcast(FP8X4), scales=scales[:], in_=tiles[i][:])
                quantised.append((codes, scales))
            return quantised

        def multiply(quantised, j, cols):
            acc = psum.tile([P, cols.stop - cols.start], F32, name="acc", tag="acc")
            for i in range(OPERANDS):
                codes, scales = quantised[i]
                nc.tensor.matmul_mx(
                    out=acc[:],
                    lhsT=codes[:, j * P : (j + 1) * P].bitcast(FP8X4),
                    lhsT_scale=scales[:, j * P : (j + 1) * P],
                    rhs=w_codes[:, i, cols].bitcast(FP8X4),
                    rhs_scale=w_scales[:, i, cols],
                    start=(i == 0),
                    stop=(i == OPERANDS - 1),
                )
            return acc

        def add_bias(sums):
            gate = gates.tile([P, ROW_TILES * N], F32, name="gate", tag="gate")
            for j in range(ROW_TILES):
                nc.vector.tensor_tensor(out=gate[:, j * N : (j + 1) * N], in0=sums[j][:], in1=bias[:], op=ADD)
            return gate

        def tanh_of_cell(r):
            cell = results.tile([P, ROW_TILES * N], F32, name="cell", tag="cell")
            nc.scalar.activation(out=cell[:], in_=loaded[0][r][:], func=TANH)
            return cell

        def sigmoid(gate):
            for j in range(ROW_TILES):
                cols = slice(j * N, (j + 1) * N)
                nc.scalar.activation(out=gate[:, cols], in_=gate[:, cols], func=SIGMOID)

        def product(r, j, gate, cell, multiplier):
            cols = slice(j * N, (j + 1) * N)
            multiplier.tensor_tensor(out=cell[:, cols], in0=gate[:, cols], in1=cell[:, cols], op=MULT)
            nc.sync.dma_start(out=rows_out[r][:, cols], in_=cell[:, cols])

        whole_tiles = [(j, slice(0, N)) for j in range(ROW_TILES)]
        last_pieces = whole_tiles[:-1] + [(ROW_TILES - 1, slice(h * N // 2, (h + 1) * N // 2)) for h in range(2)]

        cells = [tanh_of_cell(0)]
        quantised = quantise(evacuate(0, transpose(0)))
        bias = consts.tile([P, N], F32)

        for r in range(ROUNDS):
            if r + 1 < ROUNDS:
                banks = transpose(r + 1)
                cells.append(tanh_of_cell(r + 1))
            if r > 0:
                gate = add_bias(sums)
            if r + 1 < ROUNDS:
                tiles = evacuate(r + 1, banks)
            if r > 1:
                product(r - 2, 1, *finishing, nc.vector)
            pieces = whole_tiles if r + 1 < ROUNDS else last_pieces
            sums = [multiply(quantised, j, cols) for j, cols in pieces]
            if r + 1 < ROUNDS:
                quantised = quantise(tiles)
            if r == 0:
                bias_sum = psum.tile([P, N], F32, name="acc", tag="acc")
                nc.tensor.matmul(out=bias_sum[:], lhsT=ones[:], rhs=bias_rows[:], start=True, stop=True)
                nc.vector.tensor_copy(out=bias[:], in_=bias_sum[:])
            if r > 0:
                sigmoid(gate)
                product(r - 1, 0, gate, cells[r - 1], nc.gpsimd)
                finishing = (gate, cells[r - 1])
        gate = gates.tile([P, ROW_TILES * N], F32, name="gate", tag="gate")
        places = [slice(j * N + cols.start, j * N + cols.stop) for j, cols in last_pieces]
        for acc, (j, cols), there in zip(sums, last_pieces, places):
            nc.vector.tensor_tensor(out=gate[:, there], in0=acc[:], in1=bias[:, cols], op=ADD)
            nc.scalar.activation(out=gate[:, there], in_=gate[:, there], func=SIGMOID)
        product(ROUNDS - 2, 1, *finishing, nc.vector)
        cell = cells[ROUNDS - 1]
        for there in places:
            nc.vector.tensor_tensor(out=cell[:, there], in0=gate[:, there], in1=cell[:, there], op=MULT)
            nc.sync.dma_start(out=rows_out[ROUNDS - 1][:, there], in_=cell[:, there])
